import numpy as np
import ml_dtypes


def mxq(x, axis, fmt="e4m3"):
    dtype, down = {"e4m3": (ml_dtypes.float8_e4m3fn, 7), "e5m2": (ml_dtypes.float8_e5m2, 14)}[fmt]
    v = np.moveaxis(np.asarray(x, np.float32).astype(ml_dtypes.bfloat16).astype(np.float64), axis, -1)
    blocks = v.reshape(v.shape[:-1] + (-1, 32))
    amax = np.abs(blocks).max(-1, keepdims=True)
    byte = np.maximum(np.where(amax > 0, np.frexp(amax)[1] - 1 + 127, 0) - down, 1)
    scale = np.exp2(byte - 127.0)
    codes = (blocks / scale).astype(np.float32).astype(dtype).astype(np.float64)
    return np.moveaxis((codes * scale).reshape(v.shape), -1, axis)


WIDE = False


def mx_kscale(k):
    if not WIDE:
        return np.ones(k)
    levels = np.array([10, -10, 5, -5, 0])
    if k % 512:
        return np.exp2(np.random.permutation(np.resize(levels, k // 32))).repeat(32)
    a = np.empty((k // 512, 16))
    for p in range(k // 512):
        a[p, :8] = np.random.permutation(np.resize(levels, 8))
        for g in range(8):
            far = levels[np.abs(levels - a[p, g]) >= 10]
            a[p, g + 8] = far[np.random.randint(len(far))]
    return np.exp2(a.ravel()).repeat(32)


BF16 = ml_dtypes.bfloat16


def bf(x):
    return np.asarray(x, np.float32).astype(BF16)


def f64(x):
    return np.asarray(x).astype(np.float64)


B, N, D, H, DH = 1, 512, 2048, 16, 128
EPS = 1e-5


def rotate_every_two(u):
    p = u.reshape(u.shape[:-1] + (-1, 2))
    return np.stack((-p[..., 1], p[..., 0]), axis=-1).reshape(u.shape)


def apply_rotary(u, sin, cos):
    return u * cos + rotate_every_two(u) * sin


def setup_inputs():
    s = mx_kscale(D)
    r = np.exp2(-np.random.uniform(0.0, 9.0, (B, N, 1)))
    inv_freq = 1.0 / 10000.0 ** (np.arange(0, DH, 2) / DH)
    freqs = np.repeat(np.arange(N)[:, None] * inv_freq[None, :], 2, axis=-1)
    return {"x": bf((np.random.standard_normal((B, N, D)) + 0.5) * r),
            "gamma": bf((1.0 + 0.1 * np.random.standard_normal(D)) * s),
            "wq": bf(np.random.standard_normal((D, H * DH)) * 2.0 / np.sqrt(D) / s[:, None]),
            "wk": bf(np.random.standard_normal((D, DH)) / np.sqrt(D) / s[:, None]),
            "wv": bf(np.random.standard_normal((D, DH)) / np.sqrt(D) / s[:, None]),
            "sin": bf(np.sin(freqs)), "cos": bf(np.cos(freqs))}


def reference(x, gamma, wq, wk, wv, sin, cos):
    x, sin, cos = f64(x), f64(sin), f64(cos)
    mean = x.mean(-1, keepdims=True)
    var = np.square(x).mean(-1, keepdims=True) - np.square(mean)
    xn = 1.0 / np.sqrt(var + EPS) * (x - mean) * f64(gamma)
    xq = mxq(xn, 2, "e4m3")
    q = xq @ mxq(f64(wq), 0, "e4m3")
    k = xq @ mxq(f64(wk), 0, "e4m3")
    v = xq @ mxq(f64(wv), 0, "e4m3")
    q = q.reshape(B, N, H, DH).transpose(0, 2, 1, 3) * DH ** -0.5
    return apply_rotary(q, sin, cos), apply_rotary(k, sin, cos), v

@@ -1,0 +1,302 @@
+from contextlib import ExitStack
+
+import concourse.mybir as mybir
+from concourse.masks import make_identity
+
+F32 = mybir.dt.float32
+BF16 = mybir.dt.bfloat16
+U32 = mybir.dt.uint32
+U8 = mybir.dt.uint8
+FP8X4 = mybir.dt.float8_e4m3fn_x4
+ALU = mybir.AluOpType
+ACT = mybir.ActivationFunctionType
+AXIS = mybir.AxisListType
+
+P = 128
+PACK = 4
+K_PASS = P * PACK
+TOKENS = 512
+D_MODEL = 2048
+HEADS = 16
+D_HEAD = 128
+EPS = 1e-5
+
+TOKEN_TILES = TOKENS // P
+PASSES = D_MODEL // K_PASS
+ROW_GROUPS = D_MODEL // P
+PAIRS = D_HEAD // 2
+BANK = 512
+Q_CHUNKS = HEADS * D_HEAD // BANK
+HEADS_PER_CHUNK = BANK // D_HEAD
+KV = Q_CHUNKS
+CHUNKS = Q_CHUNKS + 1
+KV_WIDTH = 2 * D_HEAD
+AHEAD = 1
+REGROUPED = 2
+LOADED = 3
+RUN = 4
+VECTOR_EVERY = 8
+NORM_PASSES = 2
+
+FLOPS = 2 * TOKENS * D_MODEL * (HEADS * D_HEAD + KV_WIDTH)
+
+
+def tile_attention_pa_kernel(tc, x, gamma, wq, wk, wv, sin, cos, out_0, out_1, out_2):
+    nc = tc.nc
+    with ExitStack() as ctx:
+        keep = ctx.enter_context(tc.tile_pool(name="keep", bufs=1))
+        small = ctx.enter_context(tc.tile_pool(name="small", bufs=4))
+        rows = ctx.enter_context(tc.tile_pool(name="rows", bufs=2))
+        loaded = ctx.enter_context(tc.tile_pool(name="loaded", bufs=LOADED * PASSES))
+        regrouped = ctx.enter_context(tc.tile_pool(name="regrouped", bufs=REGROUPED * PASSES))
+        rotary = ctx.enter_context(tc.tile_pool(name="rotary", bufs=4))
+        psum = ctx.enter_context(tc.psum_pool(name="psum", bufs=8))
+        ctx.enter_context(tc.manual_schedule())
+
+        x_tiles = x.rearrange("b (t p) k -> (b t) p k", p=P)
+        x_raw = {}
+
+        def load_x(t):
+            x_raw[t] = keep.tile([P, D_MODEL], BF16, name="x_raw%d" % t)
+            nc.sync.dma_start(out=x_raw[t][:], in_=x_tiles[t])
+
+        wq_passes = wq.rearrange("(c p j) n -> c p j n", j=PACK, p=P)
+        wq_raw = {}
+
+        def load_wq(ch, c):
+            wq_raw[(ch, c)] = loaded.tile([P, PACK, BANK], BF16, name="wq_raw")
+            nc.sync.dma_start(out=wq_raw[(ch, c)][:], in_=wq_passes[c][:, :, ch * BANK : (ch + 1) * BANK])
+
+        gamma_raw = keep.tile([P, PASSES, PACK], BF16)
+        nc.scalar.dma_start(out=gamma_raw[:], in_=gamma.rearrange("(c p j) -> p c j", j=PACK, p=P))
+        for t in range(TOKEN_TILES):
+            load_x(t)
+        for c in range(PASSES):
+            load_wq(0, c)
+        cos_raw = keep.tile([P, TOKEN_TILES, D_HEAD], BF16)
+        nc.sync.dma_start(out=cos_raw[:], in_=cos.rearrange("(t p) d -> p t d", p=P))
+        sin_raw = keep.tile([P, TOKEN_TILES, D_HEAD], BF16)
+        nc.sync.dma_start(out=sin_raw[:], in_=sin.rearrange("(t p) d -> p t d", p=P))
+        for ch in range(1, LOADED):
+            for c in range(PASSES):
+                load_wq(ch, c)
+
+        kv_raw = keep.tile([P, PASSES, 2, PACK, D_HEAD], BF16)
+
+        ident_f32 = keep.tile([P, P], F32)
+        make_identity(nc, ident_f32[:])
+        ident_bf16 = keep.tile([P, P], BF16)
+        make_identity(nc, ident_bf16[:])
+        one = keep.tile([P, 1], F32)
+        nc.vector.memset(one[:], 1.0)
+        table_warm = keep.tile([P, 1], F32)
+        nc.scalar.activation(out=table_warm[:], in_=one[:], func=ACT.Sqrt)
+        mean_weights = keep.tile([P, P], BF16)
+        nc.vector.tensor_scalar(
+            out=mean_weights[:], in0=ident_bf16[:], scalar1=1.0 / D_MODEL, scalar2=None, op0=ALU.mult
+        )
+
+        def rotary_tables():
+            k_factor = keep.tile([P, TOKEN_TILES, 2, D_HEAD], F32)
+            entries = k_factor[:].rearrange("p t s (i r) -> p t s i r", r=2)
+            cos_pairs = cos_raw[:].rearrange("p t (i r) -> p t i r", r=2)
+            sin_pairs = sin_raw[:].rearrange("p t (i r) -> p t i r", r=2)
+            for s, r, source, sign in ((0, 0, cos_pairs, 1.0), (0, 1, sin_pairs, 1.0), (1, 0, sin_pairs, -1.0), (1, 1, cos_pairs, 1.0)):
+                nc.gpsimd.tensor_scalar(
+                    out=entries[:, :, s, :, r], in0=source[:, :, :, r], scalar1=sign, scalar2=0.0, op0=ALU.mult, op1=ALU.add
+                )
+            q_factor = keep.tile([P, TOKEN_TILES, 2, D_HEAD], F32)
+            nc.gpsimd.tensor_scalar(
+                out=q_factor[:], in0=k_factor[:], scalar1=D_HEAD**-0.5, scalar2=0.0, op0=ALU.mult, op1=ALU.add
+            )
+            return q_factor, k_factor
+
+        x_codes = keep.tile([P, TOKEN_TILES, PASSES, P], U32, align_bytes=64)
+        x_scales = keep.tile([P, TOKEN_TILES, PASSES, P], U8, align_bytes=64)
+        widths = [BANK] * Q_CHUNKS + [KV_WIDTH]
+        w_codes = [
+            keep.tile([P, PASSES, widths[ch]], U32, align_bytes=64, name="w_codes%d" % ch) for ch in range(CHUNKS)
+        ]
+        w_scales = [
+            keep.tile([P, PASSES, widths[ch]], U8, align_bytes=64, name="w_scales%d" % ch) for ch in range(CHUNKS)
+        ]
+
+        def fold(t):
+            folded = psum.tile([P, P], F32, tag="bank")
+            for g in range(ROW_GROUPS):
+                nc.tensor.matmul(
+                    folded[:],
+                    lhsT=mean_weights[:],
+                    rhs=x_raw[t][:, g * P : (g + 1) * P],
+                    start=(g == 0),
+                    stop=(g == ROW_GROUPS - 1),
+                )
+            return folded
+
+        def moments(t, folded):
+            squares = keep.tile([P, D_MODEL], BF16, name="squares")
+            sum_sq = small.tile([P, 1], F32)
+            nc.scalar.activation(out=squares[:], in_=x_raw[t][:], func=ACT.Square, accum_out=sum_sq[:])
+            mean = small.tile([P, 1], F32)
+            nc.vector.tensor_reduce(out=mean[:], in_=folded[:], axis=AXIS.X, op=ALU.add)
+            minus_mean = small.tile([P, 1], F32)
+            nc.vector.tensor_scalar(out=minus_mean[:], in0=mean[:], scalar1=-1.0, scalar2=None, op0=ALU.mult)
+            shift = small.tile([P, 1], F32)
+            nc.vector.tensor_scalar(
+                out=shift[:], in0=mean[:], scalar1=minus_mean[:, 0:1], scalar2=EPS, op0=ALU.mult, op1=ALU.add
+            )
+            std = small.tile([P, 1], F32)
+            nc.scalar.activation(
+                out=std[:], in_=sum_sq[:], func=ACT.Sqrt, bias=shift[:, 0:1], scale=1.0 / D_MODEL
+            )
+            return minus_mean, std
+
+        def normalise_and_transpose(t, minus_mean, std):
+            rstd = small.tile([P, 1], F32)
+            nc.vector.reciprocal(out=rstd[:], in_=std[:])
+            centred = rows.tile([P, D_MODEL], F32)
+            banks = []
+            for c in range(PASSES):
+                if c % NORM_PASSES == 0:
+                    features = slice(c * K_PASS, (c + NORM_PASSES) * K_PASS)
+                    nc.gpsimd.tensor_scalar(
+                        out=centred[:, features].rearrange("q (c j p) -> q c j p", j=PACK, p=P),
+                        in0=x_raw[t][:, features].rearrange("q (c p j) -> q c j p", j=PACK, p=P),
+                        scalar1=minus_mean[:, 0:1],
+                        scalar2=rstd[:, 0:1],
+                        op0=ALU.add,
+                        op1=ALU.mult,
+                    )
+                flipped = psum.tile([P, PACK, P], F32, tag="bank", name="flipped")
+                for j in range(PACK):
+                    g = c * PACK + j
+                    nc.tensor.transpose(flipped[:, j, :], centred[:, g * P : (g + 1) * P], ident_f32[:])
+                banks.append(flipped)
+            return banks
+
+        def scale_and_quantise(t, banks):
+            xn = rows.tile([P, PASSES, P, PACK], BF16, align_bytes=64)
+            for c in range(PASSES):
+                nc.vector.tensor_tensor(
+                    out=xn[:, c, :, :],
+                    in0=banks[c][:].rearrange("p j m -> p m j"),
+                    in1=gamma_col[:, c * PACK : (c + 1) * PACK].unsqueeze(1).to_broadcast([P, P, PACK]),
+                    op=ALU.mult,
+                )
+            nc.vector.quantize_mx(
+                out=x_codes[:, t].rearrange("p c m -> p (c m)").bitcast(FP8X4),
+                scales=x_scales[:, t].rearrange("p c m -> p (c m)"),
+                in_=xn[:].rearrange("p c m j -> p (c m j)"),
+            )
+
+        def weight_rows(ch, c):
+            if ch == KV:
+                return kv_raw[:, c].rearrange("p s j (a i) -> p s a j i", i=RUN)
+            return wq_raw[(ch, c)][:].rearrange("p j (a i) -> p a j i", i=RUN)
+
+        def regroup(ch, c):
+            grouped = regrouped.tile([P, widths[ch], PACK], BF16, tag="grouped", align_bytes=64)
+            if ch == KV:
+                target = grouped[:].rearrange("p (s a i) j -> p s a j i", s=2, i=RUN)
+            else:
+                target = grouped[:].rearrange("p (a i) j -> p a j i", i=RUN)
+            source = weight_rows(ch, c)
+            if (ch * PASSES + c) % VECTOR_EVERY == VECTOR_EVERY - 1:
+                nc.vector.tensor_copy(out=target, in_=source)
+            else:
+                nc.scalar.copy(out=target, in_=source)
+            return grouped
+
+        def quantise(ch, c, grouped):
+            nc.vector.quantize_mx(
+                out=w_codes[ch][:, c, :].bitcast(FP8X4),
+                scales=w_scales[ch][:, c, :],
+                in_=grouped[:].rearrange("p n j -> p (n j)"),
+            )
+
+        def project(ch, c, sums):
+            for t in range(TOKEN_TILES):
+                nc.tensor.matmul_mx(
+                    out=sums[t][:],
+                    lhsT=x_codes[:, t, c, :].bitcast(FP8X4),
+                    lhsT_scale=x_scales[:, t, c, :],
+                    rhs=w_codes[ch][:, c, :].bitcast(FP8X4),
+                    rhs_scale=w_scales[ch][:, c, :],
+                    start=(c == 0),
+                    stop=(c == PASSES - 1),
+                )
+
+        def rotate(result, sums, factor, n):
+            shape = [P, 2, n, PAIRS, 2]
+            products = rotary.tile([P, 2, n, D_HEAD], F32, tag="products")
+            nc.vector.tensor_tensor(
+                out=products[:].rearrange("p s n (i r) -> p s n i r", r=2),
+                in0=sums.rearrange("p n (i s) -> p s n i", s=2).unsqueeze(4).to_broadcast(shape),
+                in1=factor.rearrange("p s (i r) -> p s i r", r=2).unsqueeze(2).to_broadcast(shape),
+                op=ALU.mult,
+            )
+            nc.gpsimd.tensor_tensor(out=result, in0=products[:, 0], in1=products[:, 1], op=ALU.add)
+
+        def finish_q(ch, t, sums):
+            q_rot = rotary.tile([P, HEADS_PER_CHUNK, D_HEAD], F32, tag="q_rot")
+            rotate(q_rot[:], sums[:].rearrange("p (n d) -> p n d", d=D_HEAD), q_factor[:, t], HEADS_PER_CHUNK)
+            heads = out_0[0, ch * HEADS_PER_CHUNK : (ch + 1) * HEADS_PER_CHUNK, t * P : (t + 1) * P, :]
+            nc.sync.dma_start(out=heads.rearrange("h m d -> m h d"), in_=q_rot[:])
+
+        k_rot = keep.tile([P, TOKEN_TILES, D_HEAD], F32)
+        v_copy = keep.tile([P, TOKEN_TILES, D_HEAD], F32)
+
+        def finish_kv(t, sums):
+            rotate(k_rot[:, t : t + 1], sums[:, 0:D_HEAD].unsqueeze(1), k_factor[:, t], 1)
+            nc.scalar.copy(out=v_copy[:, t], in_=sums[:, D_HEAD:KV_WIDTH])
+
+        folds = {0: fold(0)}
+        gamma_col = keep.tile([P, ROW_GROUPS], F32)
+        nc.vector.tensor_copy(out=gamma_col[:], in_=gamma_raw[:].rearrange("p c j -> p (c j)"))
+        for t in range(1, TOKEN_TILES):
+            folds[t] = fold(t)
+        stats = {0: moments(0, folds[0])}
+        flipped_banks = {}
+        for s in range(TOKEN_TILES + 1):
+            if s < TOKEN_TILES:
+                flipped_banks[s] = normalise_and_transpose(s, stats[s][0], stats[s][1])
+            if s + 1 < TOKEN_TILES:
+                stats[s + 1] = moments(s + 1, folds[s + 1])
+            if s >= 1:
+                scale_and_quantise(s - 1, flipped_banks[s - 1])
+        q_factor, k_factor = rotary_tables()
+
+        grouped = {}
+
+        def regroup_and_reload(ch, c):
+            grouped[(ch, c)] = regroup(ch, c)
+            if ch + LOADED < Q_CHUNKS:
+                load_wq(ch + LOADED, c)
+
+        for ch in range(AHEAD):
+            for c in range(PASSES):
+                regroup_and_reload(ch, c)
+        for s, weight in enumerate((wk, wv)):
+            nc.sync.dma_start(
+                out=kv_raw[:, :, s].rearrange("p c j n -> p c (j n)"),
+                in_=weight.rearrange("(c p j) n -> p c (j n)", j=PACK, p=P),
+            )
+
+        sums = {}
+        for ch in range(CHUNKS + 1):
+            if ch < CHUNKS:
+                sums[ch] = [
+                    psum.tile([P, widths[ch]], F32, tag="bank", name="sums") for t in range(TOKEN_TILES)
+                ]
+            for i in range(PASSES):
+                if ch < CHUNKS:
+                    quantise(ch, i, grouped[(ch, i)])
+                    project(ch, i, sums[ch])
+                if ch + AHEAD < CHUNKS:
+                    regroup_and_reload(ch + AHEAD, i)
+                if 1 <= ch <= Q_CHUNKS:
+                    finish_q(ch - 1, i, sums[ch - 1][i])
+                if ch == CHUNKS:
+                    finish_kv(i, sums[KV][i])
+        nc.sync.dma_start(out=out_2[0].rearrange("(t m) d -> m t d", m=P), in_=v_copy[:])
+        nc.sync.dma_start(out=out_1[0].rearrange("(t m) d -> m t d", m=P), in_=k_rot[:])

@@ -34,7 +34,7 @@ KV_WIDTH = 2 * D_HEAD
 AHEAD = 1
 REGROUPED = 2
 LOADED = 3
-RUN = 4
+RUN = 8
 VECTOR_EVERY = 8
 NORM_PASSES = 2
 

@@ -31,12 +31,12 @@ HEADS_PER_CHUNK = BANK // D_HEAD
 KV = Q_CHUNKS
 CHUNKS = Q_CHUNKS + 1
 KV_WIDTH = 2 * D_HEAD
-AHEAD = 1
-REGROUPED = 2
-LOADED = 3
-RUN = 8
-VECTOR_EVERY = 8
+RUN = 4
+BN_TILES = 1
 NORM_PASSES = 2
+GPSIMD_UNITS = ()
+GPSIMD_COLUMNS = 128
+VECTOR_UNITS = ()
 
 FLOPS = 2 * TOKENS * D_MODEL * (HEADS * D_HEAD + KV_WIDTH)
 
@@ -47,82 +47,117 @@ def tile_attention_pa_kernel(tc, x, gamma, wq, wk, wv, sin, cos, out_0, out_1, o
         keep = ctx.enter_context(tc.tile_pool(name="keep", bufs=1))
         small = ctx.enter_context(tc.tile_pool(name="small", bufs=4))
         rows = ctx.enter_context(tc.tile_pool(name="rows", bufs=2))
-        loaded = ctx.enter_context(tc.tile_pool(name="loaded", bufs=LOADED * PASSES))
-        regrouped = ctx.enter_context(tc.tile_pool(name="regrouped", bufs=REGROUPED * PASSES))
-        rotary = ctx.enter_context(tc.tile_pool(name="rotary", bufs=4))
+        regrouped = ctx.enter_context(tc.tile_pool(name="regrouped", bufs=8))
+        coded = ctx.enter_context(tc.tile_pool(name="coded", bufs=3))
+        rotary = ctx.enter_context(tc.tile_pool(name="rotary", bufs=3))
         psum = ctx.enter_context(tc.psum_pool(name="psum", bufs=8))
         ctx.enter_context(tc.manual_schedule())
 
         x_tiles = x.rearrange("b (t p) k -> (b t) p k", p=P)
         x_raw = {}
 
-        def load_x(t):
+        def load_x(t, parts=1):
             x_raw[t] = keep.tile([P, D_MODEL], BF16, name="x_raw%d" % t)
-            nc.sync.dma_start(out=x_raw[t][:], in_=x_tiles[t])
+            width = D_MODEL // parts
+            for i in range(parts):
+                features = slice(i * width, (i + 1) * width)
+                nc.sync.dma_start(out=x_raw[t][:, features], in_=x_tiles[t][:, features])
 
         wq_passes = wq.rearrange("(c p j) n -> c p j n", j=PACK, p=P)
         wq_raw = {}
 
         def load_wq(ch, c):
-            wq_raw[(ch, c)] = loaded.tile([P, PACK, BANK], BF16, name="wq_raw")
+            wq_raw[(ch, c)] = keep.tile([P, PACK, BANK], BF16, name="wq_raw%d_%d" % (ch, c))
             nc.sync.dma_start(out=wq_raw[(ch, c)][:], in_=wq_passes[c][:, :, ch * BANK : (ch + 1) * BANK])
 
-        gamma_raw = keep.tile([P, PASSES, PACK], BF16)
-        nc.scalar.dma_start(out=gamma_raw[:], in_=gamma.rearrange("(c p j) -> p c j", j=PACK, p=P))
-        for t in range(TOKEN_TILES):
-            load_x(t)
-        for c in range(PASSES):
+        gamma_rows = keep.tile([P, K_PASS], BF16)
+        nc.vector.memset(gamma_rows[:], 0.0)
+        load_x(0, 2)
+        nc.sync.dma_start(out=gamma_rows[0:PASSES, :], in_=gamma.rearrange("(c f) -> c f", f=K_PASS))
+        load_x(1)
+        load_wq(0, 0)
+        load_x(2)
+        load_wq(0, 1)
+        load_x(3)
+        for c in range(2, PASSES):
             load_wq(0, c)
         cos_raw = keep.tile([P, TOKEN_TILES, D_HEAD], BF16)
         nc.sync.dma_start(out=cos_raw[:], in_=cos.rearrange("(t p) d -> p t d", p=P))
         sin_raw = keep.tile([P, TOKEN_TILES, D_HEAD], BF16)
         nc.sync.dma_start(out=sin_raw[:], in_=sin.rearrange("(t p) d -> p t d", p=P))
-        for ch in range(1, LOADED):
+        for ch in range(1, Q_CHUNKS):
             for c in range(PASSES):
                 load_wq(ch, c)
-
         kv_raw = keep.tile([P, PASSES, 2, PACK, D_HEAD], BF16)
+        for s, weight in enumerate((wk, wv)):
+            nc.sync.dma_start(
+                out=kv_raw[:, :, s].rearrange("p c j n -> p c (j n)"),
+                in_=weight.rearrange("(c p j) n -> p c (j n)", j=PACK, p=P),
+            )
 
-        ident_f32 = keep.tile([P, P], F32)
-        make_identity(nc, ident_f32[:])
         ident_bf16 = keep.tile([P, P], BF16)
         make_identity(nc, ident_bf16[:])
+        ident_f32 = keep.tile([P, P], F32)
+        make_identity(nc, ident_f32[:])
+        minus_half = keep.tile([P, 1], F32)
+        nc.gpsimd.memset(minus_half[:], -0.5)
         one = keep.tile([P, 1], F32)
         nc.vector.memset(one[:], 1.0)
         table_warm = keep.tile([P, 1], F32)
-        nc.scalar.activation(out=table_warm[:], in_=one[:], func=ACT.Sqrt)
+        nc.scalar.activation(out=table_warm[:], in_=one[:], func=ACT.Square)
         mean_weights = keep.tile([P, P], BF16)
         nc.vector.tensor_scalar(
-            out=mean_weights[:], in0=ident_bf16[:], scalar1=1.0 / D_MODEL, scalar2=None, op0=ALU.mult
+            out=mean_weights[:], in0=ident_bf16[:], scalar1=-1.0 / D_MODEL, scalar2=None, op0=ALU.mult
         )
+        gamma_ps = psum.tile([P, PACK, P], BF16, tag="bank", name="gamma_ps")
+        gamma_quads = gamma_rows[:].rearrange("q (p j) -> q j p", j=PACK)
+        for j in range(PACK):
+            nc.tensor.transpose(gamma_ps[:, j, :], gamma_quads[:, j, :], ident_bf16[:])
+        gamma_col = keep.tile([P, PASSES, PACK], F32)
+
+        def take_gamma():
+            nc.vector.tensor_copy(out=gamma_col[:], in_=gamma_ps[:, :, 0:PASSES].rearrange("p j c -> p c j"))
+
+        factor = keep.tile([P, TOKEN_TILES, 2, D_HEAD], BF16)
+        entries = factor[:].rearrange("p t s (i r) -> p t s i r", r=2)
+        cos_pairs = cos_raw[:].rearrange("p t (i r) -> p t i r", r=2)
+        sin_pairs = sin_raw[:].rearrange("p t (i r) -> p t i r", r=2)
+        q_factor = keep.tile([P, TOKEN_TILES, 2, D_HEAD], F32)
 
         def rotary_tables():
-            k_factor = keep.tile([P, TOKEN_TILES, 2, D_HEAD], F32)
-            entries = k_factor[:].rearrange("p t s (i r) -> p t s i r", r=2)
-            cos_pairs = cos_raw[:].rearrange("p t (i r) -> p t i r", r=2)
-            sin_pairs = sin_raw[:].rearrange("p t (i r) -> p t i r", r=2)
-            for s, r, source, sign in ((0, 0, cos_pairs, 1.0), (0, 1, sin_pairs, 1.0), (1, 0, sin_pairs, -1.0), (1, 1, cos_pairs, 1.0)):
+            for s, r, source, sign in (
+                (0, 0, cos_pairs, 1.0),
+                (0, 1, sin_pairs, 1.0),
+                (1, 0, sin_pairs, -1.0),
+                (1, 1, cos_pairs, 1.0),
+            ):
                 nc.gpsimd.tensor_scalar(
                     out=entries[:, :, s, :, r], in0=source[:, :, :, r], scalar1=sign, scalar2=0.0, op0=ALU.mult, op1=ALU.add
                 )
-            q_factor = keep.tile([P, TOKEN_TILES, 2, D_HEAD], F32)
             nc.gpsimd.tensor_scalar(
-                out=q_factor[:], in0=k_factor[:], scalar1=D_HEAD**-0.5, scalar2=0.0, op0=ALU.mult, op1=ALU.add
+                out=q_factor[:], in0=factor[:], scalar1=D_HEAD**-0.5, scalar2=0.0, op0=ALU.mult, op1=ALU.add
             )
-            return q_factor, k_factor
 
         x_codes = keep.tile([P, TOKEN_TILES, PASSES, P], U32, align_bytes=64)
         x_scales = keep.tile([P, TOKEN_TILES, PASSES, P], U8, align_bytes=64)
         widths = [BANK] * Q_CHUNKS + [KV_WIDTH]
-        w_codes = [
-            keep.tile([P, PASSES, widths[ch]], U32, align_bytes=64, name="w_codes%d" % ch) for ch in range(CHUNKS)
-        ]
-        w_scales = [
-            keep.tile([P, PASSES, widths[ch]], U8, align_bytes=64, name="w_scales%d" % ch) for ch in range(CHUNKS)
-        ]
+        w_codes = {}
+        w_scales = {}
 
-        def fold(t):
-            folded = psum.tile([P, P], F32, tag="bank")
+        def vector_moments(t):
+            stats = small.tile([P, PASSES, 6], F32, name="stats")
+            for c in range(PASSES):
+                nc.vector.bn_stats(out=stats[:, c], in_=x_raw[t][:, c * K_PASS : (c + 1) * K_PASS])
+            moments = small.tile([P, 2], F32, name="moments")
+            nc.vector.bn_aggr(out=moments[:], in_=stats[:].rearrange("p c s -> p (c s)"))
+            var_eps = small.tile([P, 1], F32, name="var_eps")
+            nc.vector.tensor_scalar(out=var_eps[:], in0=moments[:, 1:2], scalar1=EPS, scalar2=None, op0=ALU.add)
+            minus_mean = small.tile([P, 1], F32, name="minus_mean")
+            nc.vector.tensor_scalar(out=minus_mean[:], in0=moments[:, 0:1], scalar1=-1.0, scalar2=None, op0=ALU.mult)
+            return minus_mean, var_eps
+
+        def fold_and_square(t):
+            folded = psum.tile([P, P], F32, tag="bank", name="folded")
             for g in range(ROW_GROUPS):
                 nc.tensor.matmul(
                     folded[:],
@@ -131,35 +166,35 @@ def tile_attention_pa_kernel(tc, x, gamma, wq, wk, wv, sin, cos, out_0, out_1, o
                     start=(g == 0),
                     stop=(g == ROW_GROUPS - 1),
                 )
-            return folded
-
-        def moments(t, folded):
             squares = keep.tile([P, D_MODEL], BF16, name="squares")
-            sum_sq = small.tile([P, 1], F32)
+            sum_sq = small.tile([P, 1], F32, name="sum_sq")
             nc.scalar.activation(out=squares[:], in_=x_raw[t][:], func=ACT.Square, accum_out=sum_sq[:])
-            mean = small.tile([P, 1], F32)
-            nc.vector.tensor_reduce(out=mean[:], in_=folded[:], axis=AXIS.X, op=ALU.add)
-            minus_mean = small.tile([P, 1], F32)
-            nc.vector.tensor_scalar(out=minus_mean[:], in0=mean[:], scalar1=-1.0, scalar2=None, op0=ALU.mult)
-            shift = small.tile([P, 1], F32)
-            nc.vector.tensor_scalar(
-                out=shift[:], in0=mean[:], scalar1=minus_mean[:, 0:1], scalar2=EPS, op0=ALU.mult, op1=ALU.add
-            )
-            std = small.tile([P, 1], F32)
-            nc.scalar.activation(
-                out=std[:], in_=sum_sq[:], func=ACT.Sqrt, bias=shift[:, 0:1], scale=1.0 / D_MODEL
-            )
-            return minus_mean, std
+            return folded, sum_sq
 
-        def normalise_and_transpose(t, minus_mean, std):
-            rstd = small.tile([P, 1], F32)
-            nc.vector.reciprocal(out=rstd[:], in_=std[:])
-            centred = rows.tile([P, D_MODEL], F32)
+        def scalar_moments(folded, sum_sq):
+            minus_mean = small.tile([P, 1], F32, name="minus_mean")
+            nc.vector.tensor_reduce(out=minus_mean[:], in_=folded[:], axis=AXIS.X, op=ALU.add)
+            shift = small.tile([P, 1], F32, name="shift")
+            nc.vector.tensor_scalar(
+                out=shift[:], in0=minus_mean[:], scalar1=minus_mean[:, 0:1], scalar2=EPS, op0=ALU.mult, op1=ALU.subtract
+            )
+            var_eps = small.tile([P, 1], F32, name="var_eps")
+            nc.gpsimd.tensor_scalar(
+                out=var_eps[:], in0=sum_sq[:], scalar1=1.0 / D_MODEL, scalar2=shift[:, 0:1], op0=ALU.mult, op1=ALU.subtract
+            )
+            return minus_mean, var_eps
+
+        def normalise_and_transpose(t, minus_mean, var_eps):
+            rstd = small.tile([P, 1], F32, name="rstd")
+            nc.gpsimd.tensor_tensor(out=rstd[:], in0=var_eps[:], in1=minus_half[:], op=ALU.pow)
+            centred = rows.tile([P, D_MODEL], F32, name="centred")
+            engine = nc.vector if t == 0 else nc.gpsimd
+            passes = 1 if t == 0 else NORM_PASSES
             banks = []
             for c in range(PASSES):
-                if c % NORM_PASSES == 0:
-                    features = slice(c * K_PASS, (c + NORM_PASSES) * K_PASS)
-                    nc.gpsimd.tensor_scalar(
+                if c % passes == 0:
+                    features = slice(c * K_PASS, (c + passes) * K_PASS)
+                    engine.tensor_scalar(
                         out=centred[:, features].rearrange("q (c j p) -> q c j p", j=PACK, p=P),
                         in0=x_raw[t][:, features].rearrange("q (c p j) -> q c j p", j=PACK, p=P),
                         scalar1=minus_mean[:, 0:1],
@@ -174,129 +209,172 @@ def tile_attention_pa_kernel(tc, x, gamma, wq, wk, wv, sin, cos, out_0, out_1, o
                 banks.append(flipped)
             return banks
 
-        def scale_and_quantise(t, banks):
-            xn = rows.tile([P, PASSES, P, PACK], BF16, align_bytes=64)
+        def scale(t, banks):
+            xn = rows.tile([P, PASSES, P, PACK], BF16, align_bytes=64, name="xn")
             for c in range(PASSES):
                 nc.vector.tensor_tensor(
                     out=xn[:, c, :, :],
                     in0=banks[c][:].rearrange("p j m -> p m j"),
-                    in1=gamma_col[:, c * PACK : (c + 1) * PACK].unsqueeze(1).to_broadcast([P, P, PACK]),
+                    in1=gamma_col[:, c, :].unsqueeze(1).to_broadcast([P, P, PACK]),
                     op=ALU.mult,
                 )
+            return xn
+
+        def quantise_x(t, xn):
             nc.vector.quantize_mx(
                 out=x_codes[:, t].rearrange("p c m -> p (c m)").bitcast(FP8X4),
                 scales=x_scales[:, t].rearrange("p c m -> p (c m)"),
                 in_=xn[:].rearrange("p c m j -> p (c m j)"),
             )
 
-        def weight_rows(ch, c):
-            if ch == KV:
-                return kv_raw[:, c].rearrange("p s j (a i) -> p s a j i", i=RUN)
-            return wq_raw[(ch, c)][:].rearrange("p j (a i) -> p a j i", i=RUN)
+        grouped = {}
 
         def regroup(ch, c):
-            grouped = regrouped.tile([P, widths[ch], PACK], BF16, tag="grouped", align_bytes=64)
-            if ch == KV:
-                target = grouped[:].rearrange("p (s a i) j -> p s a j i", s=2, i=RUN)
+            grouped[(ch, c)] = regrouped.tile(
+                [P, widths[ch], PACK], BF16, tag="grouped", align_bytes=64, name="grouped"
+            )
+            if (ch, c) in GPSIMD_UNITS:
+                piece = GPSIMD_COLUMNS
+                for n0 in range(0, BANK, piece):
+                    nc.gpsimd.tensor_scalar(
+                        out=grouped[(ch, c)][:, n0 : n0 + piece, :],
+                        in0=wq_raw[(ch, c)][:, :, n0 : n0 + piece].rearrange("p j n -> p n j"),
+                        scalar1=1.0,
+                        scalar2=0.0,
+                        op0=ALU.mult,
+                        op1=ALU.add,
+                    )
+            elif (ch, c) in VECTOR_UNITS:
+                nc.vector.tensor_copy(
+                    out=grouped[(ch, c)][:].rearrange("p (a i) j -> p a j i", i=RUN),
+                    in_=wq_raw[(ch, c)][:].rearrange("p j (a i) -> p a j i", i=RUN),
+                )
+            elif ch == KV:
+                nc.scalar.copy(
+                    out=grouped[(ch, c)][:].rearrange("p (s a i) j -> p s a j i", s=2, i=RUN),
+                    in_=kv_raw[:, c].rearrange("p s j (a i) -> p s a j i", i=RUN),
+                )
             else:
-                target = grouped[:].rearrange("p (a i) j -> p a j i", i=RUN)
-            source = weight_rows(ch, c)
-            if (ch * PASSES + c) % VECTOR_EVERY == VECTOR_EVERY - 1:
-                nc.vector.tensor_copy(out=target, in_=source)
-            else:
-                nc.scalar.copy(out=target, in_=source)
-            return grouped
+                nc.scalar.copy(
+                    out=grouped[(ch, c)][:].rearrange("p (a i) j -> p a j i", i=RUN),
+                    in_=wq_raw[(ch, c)][:].rearrange("p j (a i) -> p a j i", i=RUN),
+                )
 
-        def quantise(ch, c, grouped):
+        def quantise(ch, c):
+            if c == 0:
+                w_codes[ch] = coded.tile([P, PASSES, widths[ch]], U32, tag="codes", align_bytes=64, name="w_codes")
+                w_scales[ch] = coded.tile([P, PASSES, widths[ch]], U8, tag="scales", align_bytes=64, name="w_scales")
             nc.vector.quantize_mx(
                 out=w_codes[ch][:, c, :].bitcast(FP8X4),
                 scales=w_scales[ch][:, c, :],
-                in_=grouped[:].rearrange("p n j -> p (n j)"),
+                in_=grouped[(ch, c)][:].rearrange("p n j -> p (n j)"),
             )
 
-        def project(ch, c, sums):
-            for t in range(TOKEN_TILES):
+        def project(out, ch, t, columns):
+            for c in range(PASSES):
                 nc.tensor.matmul_mx(
-                    out=sums[t][:],
+                    out=out,
                     lhsT=x_codes[:, t, c, :].bitcast(FP8X4),
                     lhsT_scale=x_scales[:, t, c, :],
-                    rhs=w_codes[ch][:, c, :].bitcast(FP8X4),
-                    rhs_scale=w_scales[ch][:, c, :],
+                    rhs=w_codes[ch][:, c, columns].bitcast(FP8X4),
+                    rhs_scale=w_scales[ch][:, c, columns],
                     start=(c == 0),
                     stop=(c == PASSES - 1),
                 )
 
-        def rotate(result, sums, factor, n):
-            shape = [P, 2, n, PAIRS, 2]
-            products = rotary.tile([P, 2, n, D_HEAD], F32, tag="products")
+        sums = {}
+
+        def project_q(ch, t):
+            sums[(ch, t)] = psum.tile([P, BANK], F32, tag="bank", name="sums")
+            project(sums[(ch, t)][:], ch, t, slice(0, BANK))
+
+        def finish_q(ch, t):
+            shape = [P, 2, HEADS_PER_CHUNK, PAIRS, 2]
+            products = rotary.tile([P, 2, HEADS_PER_CHUNK, D_HEAD], F32, tag="products", name="products")
             nc.vector.tensor_tensor(
                 out=products[:].rearrange("p s n (i r) -> p s n i r", r=2),
-                in0=sums.rearrange("p n (i s) -> p s n i", s=2).unsqueeze(4).to_broadcast(shape),
-                in1=factor.rearrange("p s (i r) -> p s i r", r=2).unsqueeze(2).to_broadcast(shape),
+                in0=sums[(ch, t)][:]
+                .rearrange("p (n i s) -> p s n i", s=2, i=PAIRS)
+                .unsqueeze(4)
+                .to_broadcast(shape),
+                in1=q_factor[:, t].rearrange("p s (i r) -> p s i r", r=2).unsqueeze(2).to_broadcast(shape),
                 op=ALU.mult,
             )
-            nc.gpsimd.tensor_tensor(out=result, in0=products[:, 0], in1=products[:, 1], op=ALU.add)
-
-        def finish_q(ch, t, sums):
-            q_rot = rotary.tile([P, HEADS_PER_CHUNK, D_HEAD], F32, tag="q_rot")
-            rotate(q_rot[:], sums[:].rearrange("p (n d) -> p n d", d=D_HEAD), q_factor[:, t], HEADS_PER_CHUNK)
+            q_rot = rotary.tile([P, HEADS_PER_CHUNK, D_HEAD], F32, tag="q_rot", name="q_rot", bufs=5)
+            nc.gpsimd.tensor_tensor(out=q_rot[:], in0=products[:, 0], in1=products[:, 1], op=ALU.add)
             heads = out_0[0, ch * HEADS_PER_CHUNK : (ch + 1) * HEADS_PER_CHUNK, t * P : (t + 1) * P, :]
             nc.sync.dma_start(out=heads.rearrange("h m d -> m h d"), in_=q_rot[:])
 
-        k_rot = keep.tile([P, TOKEN_TILES, D_HEAD], F32)
+        def project_kv(c):
+            for t in range(TOKEN_TILES):
+                if c == 0:
+                    sums[(KV, t)] = psum.tile([P, KV_WIDTH], F32, tag="bank", name="sums")
+                nc.tensor.matmul_mx(
+                    out=sums[(KV, t)][:],
+                    lhsT=x_codes[:, t, c, :].bitcast(FP8X4),
+                    lhsT_scale=x_scales[:, t, c, :],
+                    rhs=w_codes[KV][:, c, :].bitcast(FP8X4),
+                    rhs_scale=w_scales[KV][:, c, :],
+                    start=(c == 0),
+                    stop=(c == PASSES - 1),
+                )
+
         v_copy = keep.tile([P, TOKEN_TILES, D_HEAD], F32)
+        k_rot = keep.tile([P, TOKEN_TILES, D_HEAD], F32)
 
-        def finish_kv(t, sums):
-            rotate(k_rot[:, t : t + 1], sums[:, 0:D_HEAD].unsqueeze(1), k_factor[:, t], 1)
-            nc.scalar.copy(out=v_copy[:, t], in_=sums[:, D_HEAD:KV_WIDTH])
-
-        folds = {0: fold(0)}
-        gamma_col = keep.tile([P, ROW_GROUPS], F32)
-        nc.vector.tensor_copy(out=gamma_col[:], in_=gamma_raw[:].rearrange("p c j -> p (c j)"))
-        for t in range(1, TOKEN_TILES):
-            folds[t] = fold(t)
-        stats = {0: moments(0, folds[0])}
-        flipped_banks = {}
-        for s in range(TOKEN_TILES + 1):
-            if s < TOKEN_TILES:
-                flipped_banks[s] = normalise_and_transpose(s, stats[s][0], stats[s][1])
-            if s + 1 < TOKEN_TILES:
-                stats[s + 1] = moments(s + 1, folds[s + 1])
-            if s >= 1:
-                scale_and_quantise(s - 1, flipped_banks[s - 1])
-        q_factor, k_factor = rotary_tables()
-
-        grouped = {}
-
-        def regroup_and_reload(ch, c):
-            grouped[(ch, c)] = regroup(ch, c)
-            if ch + LOADED < Q_CHUNKS:
-                load_wq(ch + LOADED, c)
-
-        for ch in range(AHEAD):
-            for c in range(PASSES):
-                regroup_and_reload(ch, c)
-        for s, weight in enumerate((wk, wv)):
-            nc.sync.dma_start(
-                out=kv_raw[:, :, s].rearrange("p c j n -> p c (j n)"),
-                in_=weight.rearrange("(c p j) n -> p c (j n)", j=PACK, p=P),
+        def finish_kv(t):
+            shape = [P, 2, PAIRS, 2]
+            products = rotary.tile([P, 2, D_HEAD], F32, tag="k_products", name="k_products")
+            nc.vector.tensor_tensor(
+                out=products[:].rearrange("p s (i r) -> p s i r", r=2),
+                in0=sums[(KV, t)][:, 0:D_HEAD].rearrange("p (i s) -> p s i", s=2).unsqueeze(3).to_broadcast(shape),
+                in1=factor[:, t].rearrange("p s (i r) -> p s i r", r=2),
+                op=ALU.mult,
             )
+            nc.gpsimd.tensor_tensor(out=k_rot[:, t], in0=products[:, 0], in1=products[:, 1], op=ALU.add)
+            nc.scalar.copy(out=v_copy[:, t], in_=sums[(KV, t)][:, D_HEAD:KV_WIDTH])
 
-        sums = {}
-        for ch in range(CHUNKS + 1):
-            if ch < CHUNKS:
-                sums[ch] = [
-                    psum.tile([P, widths[ch]], F32, tag="bank", name="sums") for t in range(TOKEN_TILES)
-                ]
-            for i in range(PASSES):
-                if ch < CHUNKS:
-                    quantise(ch, i, grouped[(ch, i)])
-                    project(ch, i, sums[ch])
-                if ch + AHEAD < CHUNKS:
-                    regroup_and_reload(ch + AHEAD, i)
-                if 1 <= ch <= Q_CHUNKS:
-                    finish_q(ch - 1, i, sums[ch - 1][i])
-                if ch == CHUNKS:
-                    finish_kv(i, sums[KV][i])
+        banks = {}
+        partial = {}
+        moments = {0: vector_moments(0)}
+        for t in range(1, TOKEN_TILES):
+            partial[t] = fold_and_square(t)
+            if t == 1:
+                banks[0] = normalise_and_transpose(0, moments[0][0], moments[0][1])
+                take_gamma()
+        for c in range(PASSES):
+            regroup(0, c)
+        moments[1] = scalar_moments(partial[1][0], partial[1][1])
+        for t in range(TOKEN_TILES):
+            if t + 1 < TOKEN_TILES:
+                banks[t + 1] = normalise_and_transpose(t + 1, moments[t + 1][0], moments[t + 1][1])
+            xn = scale(t, banks[t])
+            if t + 2 < TOKEN_TILES:
+                moments[t + 2] = scalar_moments(partial[t + 2][0], partial[t + 2][1])
+            quantise_x(t, xn)
+            if t >= 2:
+                quantise(0, t - 2)
+        rotary_tables()
+        quantise(0, 2)
+        quantise(0, 3)
+        regroup(1, 0)
+
+        for t in range(TOKEN_TILES):
+            project_q(0, t)
+        for c in range(1, PASSES):
+            regroup(1, c)
+        for ch in range(Q_CHUNKS):
+            for t in range(TOKEN_TILES):
+                quantise(ch + 1, t)
+                if ch + 2 < CHUNKS:
+                    regroup(ch + 2, t)
+                finish_q(ch, t)
+            if ch + 1 < KV:
+                for t in range(TOKEN_TILES):
+                    project_q(ch + 1, t)
+        for c in range(PASSES):
+            project_kv(c)
+        for t in range(TOKEN_TILES):
+            finish_kv(t)
         nc.sync.dma_start(out=out_2[0].rearrange("(t m) d -> m t d", m=P), in_=v_copy[:])
         nc.sync.dma_start(out=out_1[0].rearrange("(t m) d -> m t d", m=P), in_=k_rot[:])

@@ -31,12 +31,11 @@ HEADS_PER_CHUNK = BANK // D_HEAD
 KV = Q_CHUNKS
 CHUNKS = Q_CHUNKS + 1
 KV_WIDTH = 2 * D_HEAD
+LEAD = 3
 RUN = 4
-BN_TILES = 1
+BN_TILES = 2
 NORM_PASSES = 2
-GPSIMD_UNITS = ()
-GPSIMD_COLUMNS = 128
-VECTOR_UNITS = ()
+VECTOR_UNITS = ((0, 3),)
 
 FLOPS = 2 * TOKENS * D_MODEL * (HEADS * D_HEAD + KV_WIDTH)
 
@@ -72,19 +71,16 @@ def tile_attention_pa_kernel(tc, x, gamma, wq, wk, wv, sin, cos, out_0, out_1, o
 
         gamma_rows = keep.tile([P, K_PASS], BF16)
         nc.vector.memset(gamma_rows[:], 0.0)
-        load_x(0, 2)
+        load_x(0, 4)
         nc.sync.dma_start(out=gamma_rows[0:PASSES, :], in_=gamma.rearrange("(c f) -> c f", f=K_PASS))
-        load_x(1)
-        load_wq(0, 0)
-        load_x(2)
-        load_wq(0, 1)
-        load_x(3)
-        for c in range(2, PASSES):
-            load_wq(0, c)
         cos_raw = keep.tile([P, TOKEN_TILES, D_HEAD], BF16)
         nc.sync.dma_start(out=cos_raw[:], in_=cos.rearrange("(t p) d -> p t d", p=P))
         sin_raw = keep.tile([P, TOKEN_TILES, D_HEAD], BF16)
         nc.sync.dma_start(out=sin_raw[:], in_=sin.rearrange("(t p) d -> p t d", p=P))
+        for t in range(1, TOKEN_TILES):
+            load_x(t)
+        for c in range(PASSES):
+            load_wq(0, c)
         for ch in range(1, Q_CHUNKS):
             for c in range(PASSES):
                 load_wq(ch, c)
@@ -131,12 +127,8 @@ def tile_attention_pa_kernel(tc, x, gamma, wq, wk, wv, sin, cos, out_0, out_1, o
                 (1, 0, sin_pairs, -1.0),
                 (1, 1, cos_pairs, 1.0),
             ):
-                nc.gpsimd.tensor_scalar(
-                    out=entries[:, :, s, :, r], in0=source[:, :, :, r], scalar1=sign, scalar2=0.0, op0=ALU.mult, op1=ALU.add
-                )
-            nc.gpsimd.tensor_scalar(
-                out=q_factor[:], in0=factor[:], scalar1=D_HEAD**-0.5, scalar2=0.0, op0=ALU.mult, op1=ALU.add
-            )
+                nc.scalar.activation(out=entries[:, :, s, :, r], in_=source[:, :, :, r], func=ACT.Copy, scale=sign)
+            nc.scalar.activation(out=q_factor[:], in_=factor[:], func=ACT.Copy, scale=D_HEAD**-0.5)
 
         x_codes = keep.tile([P, TOKEN_TILES, PASSES, P], U32, align_bytes=64)
         x_scales = keep.tile([P, TOKEN_TILES, PASSES, P], U8, align_bytes=64)
@@ -188,7 +180,7 @@ def tile_attention_pa_kernel(tc, x, gamma, wq, wk, wv, sin, cos, out_0, out_1, o
             rstd = small.tile([P, 1], F32, name="rstd")
             nc.gpsimd.tensor_tensor(out=rstd[:], in0=var_eps[:], in1=minus_half[:], op=ALU.pow)
             centred = rows.tile([P, D_MODEL], F32, name="centred")
-            engine = nc.vector if t == 0 else nc.gpsimd
+            engine = nc.gpsimd
             passes = 1 if t == 0 else NORM_PASSES
             banks = []
             for c in range(PASSES):
@@ -233,18 +225,7 @@ def tile_attention_pa_kernel(tc, x, gamma, wq, wk, wv, sin, cos, out_0, out_1, o
             grouped[(ch, c)] = regrouped.tile(
                 [P, widths[ch], PACK], BF16, tag="grouped", align_bytes=64, name="grouped"
             )
-            if (ch, c) in GPSIMD_UNITS:
-                piece = GPSIMD_COLUMNS
-                for n0 in range(0, BANK, piece):
-                    nc.gpsimd.tensor_scalar(
-                        out=grouped[(ch, c)][:, n0 : n0 + piece, :],
-                        in0=wq_raw[(ch, c)][:, :, n0 : n0 + piece].rearrange("p j n -> p n j"),
-                        scalar1=1.0,
-                        scalar2=0.0,
-                        op0=ALU.mult,
-                        op1=ALU.add,
-                    )
-            elif (ch, c) in VECTOR_UNITS:
+            if (ch, c) in VECTOR_UNITS:
                 nc.vector.tensor_copy(
                     out=grouped[(ch, c)][:].rearrange("p (a i) j -> p a j i", i=RUN),
                     in_=wq_raw[(ch, c)][:].rearrange("p j (a i) -> p a j i", i=RUN),
@@ -320,61 +301,70 @@ def tile_attention_pa_kernel(tc, x, gamma, wq, wk, wv, sin, cos, out_0, out_1, o
                 )
 
         v_copy = keep.tile([P, TOKEN_TILES, D_HEAD], F32)
-        k_rot = keep.tile([P, TOKEN_TILES, D_HEAD], F32)
 
-        def finish_kv(t):
-            shape = [P, 2, PAIRS, 2]
-            products = rotary.tile([P, 2, D_HEAD], F32, tag="k_products", name="k_products")
-            nc.vector.tensor_tensor(
-                out=products[:].rearrange("p s (i r) -> p s i r", r=2),
-                in0=sums[(KV, t)][:, 0:D_HEAD].rearrange("p (i s) -> p s i", s=2).unsqueeze(3).to_broadcast(shape),
-                in1=factor[:, t].rearrange("p s (i r) -> p s i r", r=2),
-                op=ALU.mult,
-            )
-            nc.gpsimd.tensor_tensor(out=k_rot[:, t], in0=products[:, 0], in1=products[:, 1], op=ALU.add)
-            nc.scalar.copy(out=v_copy[:, t], in_=sums[(KV, t)][:, D_HEAD:KV_WIDTH])
+        def finish_kv():
+            products = rotary.tile([P, 2, TOKEN_TILES, D_HEAD], F32, tag="products", name="products")
+            for t in range(TOKEN_TILES):
+                shape = [P, 2, PAIRS, 2]
+                nc.vector.tensor_tensor(
+                    out=products[:, :, t].rearrange("p s (i r) -> p s i r", r=2),
+                    in0=sums[(KV, t)][:, 0:D_HEAD].rearrange("p (i s) -> p s i", s=2).unsqueeze(3).to_broadcast(shape),
+                    in1=factor[:, t].rearrange("p s (i r) -> p s i r", r=2),
+                    op=ALU.mult,
+                )
+                nc.scalar.copy(out=v_copy[:, t], in_=sums[(KV, t)][:, D_HEAD:KV_WIDTH])
+            nc.sync.dma_start(out=out_2[0].rearrange("(t m) d -> m t d", m=P), in_=v_copy[:])
+            k_rot = rotary.tile([P, TOKEN_TILES, D_HEAD], F32, tag="q_rot", name="k_rot", bufs=5)
+            nc.vector.tensor_tensor(out=k_rot[:], in0=products[:, 0], in1=products[:, 1], op=ALU.add)
+            nc.sync.dma_start(out=out_1[0].rearrange("(t m) d -> m t d", m=P), in_=k_rot[:])
 
         banks = {}
         partial = {}
-        moments = {0: vector_moments(0)}
-        for t in range(1, TOKEN_TILES):
-            partial[t] = fold_and_square(t)
-            if t == 1:
-                banks[0] = normalise_and_transpose(0, moments[0][0], moments[0][1])
-                take_gamma()
-        for c in range(PASSES):
-            regroup(0, c)
-        moments[1] = scalar_moments(partial[1][0], partial[1][1])
-        for t in range(TOKEN_TILES):
-            if t + 1 < TOKEN_TILES:
-                banks[t + 1] = normalise_and_transpose(t + 1, moments[t + 1][0], moments[t + 1][1])
-            xn = scale(t, banks[t])
-            if t + 2 < TOKEN_TILES:
-                moments[t + 2] = scalar_moments(partial[t + 2][0], partial[t + 2][1])
-            quantise_x(t, xn)
-            if t >= 2:
-                quantise(0, t - 2)
         rotary_tables()
+        banks = {}
+        partial = {}
+        xn = {}
+        moments = {0: vector_moments(0)}
+        banks[0] = normalise_and_transpose(0, moments[0][0], moments[0][1])
+        moments[1] = vector_moments(1)
+        take_gamma()
+        partial[2] = fold_and_square(2)
+        banks[1] = normalise_and_transpose(1, moments[1][0], moments[1][1])
+        xn[0] = scale(0, banks[0])
+        moments[2] = scalar_moments(partial[2][0], partial[2][1])
+        quantise_x(0, xn[0])
+        partial[3] = fold_and_square(3)
+        for c in range(3):
+            regroup(0, c)
+        banks[2] = normalise_and_transpose(2, moments[2][0], moments[2][1])
+        xn[1] = scale(1, banks[1])
+        moments[3] = scalar_moments(partial[3][0], partial[3][1])
+        quantise_x(1, xn[1])
+        banks[3] = normalise_and_transpose(3, moments[3][0], moments[3][1])
+        regroup(0, 3)
+        xn[2] = scale(2, banks[2])
+        quantise(0, 0)
+        quantise_x(2, xn[2])
+        xn[3] = scale(3, banks[3])
+        quantise(0, 1)
+        quantise_x(3, xn[3])
         quantise(0, 2)
         quantise(0, 3)
-        regroup(1, 0)
+        later = [(ch, c) for ch in range(1, CHUNKS) for c in range(PASSES)]
+        for unit in later[:LEAD]:
+            regroup(unit[0], unit[1])
 
         for t in range(TOKEN_TILES):
             project_q(0, t)
-        for c in range(1, PASSES):
-            regroup(1, c)
         for ch in range(Q_CHUNKS):
             for t in range(TOKEN_TILES):
                 quantise(ch + 1, t)
-                if ch + 2 < CHUNKS:
-                    regroup(ch + 2, t)
+                for unit in later[ch * PASSES + t + LEAD :][:1]:
+                    regroup(unit[0], unit[1])
                 finish_q(ch, t)
             if ch + 1 < KV:
                 for t in range(TOKEN_TILES):
                     project_q(ch + 1, t)
         for c in range(PASSES):
             project_kv(c)
-        for t in range(TOKEN_TILES):
-            finish_kv(t)
-        nc.sync.dma_start(out=out_2[0].rearrange("(t m) d -> m t d", m=P), in_=v_copy[:])
-        nc.sync.dma_start(out=out_1[0].rearrange("(t m) d -> m t d", m=P), in_=k_rot[:])
+        finish_kv()

@@ -31,6 +31,7 @@ HEADS_PER_CHUNK = BANK // D_HEAD
 KV = Q_CHUNKS
 CHUNKS = Q_CHUNKS + 1
 KV_WIDTH = 2 * D_HEAD
+LOAD_COLUMNS = 2 * BANK
 LEAD = 3
 RUN = 4
 BN_TILES = 2
@@ -65,9 +66,10 @@ def tile_attention_pa_kernel(tc, x, gamma, wq, wk, wv, sin, cos, out_0, out_1, o
         wq_passes = wq.rearrange("(c p j) n -> c p j n", j=PACK, p=P)
         wq_raw = {}
 
-        def load_wq(ch, c):
-            wq_raw[(ch, c)] = keep.tile([P, PACK, BANK], BF16, name="wq_raw%d_%d" % (ch, c))
-            nc.sync.dma_start(out=wq_raw[(ch, c)][:], in_=wq_passes[c][:, :, ch * BANK : (ch + 1) * BANK])
+        def load_wq(part, c):
+            wq_raw[(part, c)] = keep.tile([P, PACK, LOAD_COLUMNS], BF16, name="wq_raw%d_%d" % (part, c))
+            columns = slice(part * LOAD_COLUMNS, (part + 1) * LOAD_COLUMNS)
+            nc.sync.dma_start(out=wq_raw[(part, c)][:], in_=wq_passes[c][:, :, columns])
 
         gamma_rows = keep.tile([P, K_PASS], BF16)
         nc.vector.memset(gamma_rows[:], 0.0)
@@ -79,11 +81,9 @@ def tile_attention_pa_kernel(tc, x, gamma, wq, wk, wv, sin, cos, out_0, out_1, o
         nc.sync.dma_start(out=sin_raw[:], in_=sin.rearrange("(t p) d -> p t d", p=P))
         for t in range(1, TOKEN_TILES):
             load_x(t)
-        for c in range(PASSES):
-            load_wq(0, c)
-        for ch in range(1, Q_CHUNKS):
+        for part in range(HEADS * D_HEAD // LOAD_COLUMNS):
             for c in range(PASSES):
-                load_wq(ch, c)
+                load_wq(part, c)
         kv_raw = keep.tile([P, PASSES, 2, PACK, D_HEAD], BF16)
         for s, weight in enumerate((wk, wv)):
             nc.sync.dma_start(
@@ -221,6 +221,10 @@ def tile_attention_pa_kernel(tc, x, gamma, wq, wk, wv, sin, cos, out_0, out_1, o
 
         grouped = {}
 
+        def loaded_rows(ch, c):
+            part, first = divmod(ch * BANK, LOAD_COLUMNS)
+            return wq_raw[(part, c)][:, :, first : first + BANK]
+
         def regroup(ch, c):
             grouped[(ch, c)] = regrouped.tile(
                 [P, widths[ch], PACK], BF16, tag="grouped", align_bytes=64, name="grouped"
@@ -228,7 +232,7 @@ def tile_attention_pa_kernel(tc, x, gamma, wq, wk, wv, sin, cos, out_0, out_1, o
             if (ch, c) in VECTOR_UNITS:
                 nc.vector.tensor_copy(
                     out=grouped[(ch, c)][:].rearrange("p (a i) j -> p a j i", i=RUN),
-                    in_=wq_raw[(ch, c)][:].rearrange("p j (a i) -> p a j i", i=RUN),
+                    in_=loaded_rows(ch, c).rearrange("p j (a i) -> p a j i", i=RUN),
                 )
             elif ch == KV:
                 nc.scalar.copy(
@@ -238,7 +242,7 @@ def tile_attention_pa_kernel(tc, x, gamma, wq, wk, wv, sin, cos, out_0, out_1, o
             else:
                 nc.scalar.copy(
                     out=grouped[(ch, c)][:].rearrange("p (a i) j -> p a j i", i=RUN),
-                    in_=wq_raw[(ch, c)][:].rearrange("p j (a i) -> p a j i", i=RUN),
+                    in_=loaded_rows(ch, c).rearrange("p j (a i) -> p a j i", i=RUN),
                 )
 
         def quantise(ch, c):

@@ -31,12 +31,13 @@ HEADS_PER_CHUNK = BANK // D_HEAD
 KV = Q_CHUNKS
 CHUNKS = Q_CHUNKS + 1
 KV_WIDTH = 2 * D_HEAD
+STORED_TILES = 2
 LOAD_COLUMNS = 2 * BANK
 LEAD = 3
 RUN = 4
 BN_TILES = 2
 NORM_PASSES = 2
-VECTOR_UNITS = ((0, 3),)
+VECTOR_UNITS = ((1, 2),)
 
 FLOPS = 2 * TOKENS * D_MODEL * (HEADS * D_HEAD + KV_WIDTH)
 
@@ -53,7 +54,7 @@ def tile_attention_pa_kernel(tc, x, gamma, wq, wk, wv, sin, cos, out_0, out_1, o
         psum = ctx.enter_context(tc.psum_pool(name="psum", bufs=8))
         ctx.enter_context(tc.manual_schedule())
 
-        x_tiles = x.rearrange("b (t p) k -> (b t) p k", p=P)
+        x_tiles = x.rearrange("b (p t) k -> (b t) p k", p=P)
         x_raw = {}
 
         def load_x(t, parts=1):
@@ -76,9 +77,9 @@ def tile_attention_pa_kernel(tc, x, gamma, wq, wk, wv, sin, cos, out_0, out_1, o
         load_x(0, 4)
         nc.sync.dma_start(out=gamma_rows[0:PASSES, :], in_=gamma.rearrange("(c f) -> c f", f=K_PASS))
         cos_raw = keep.tile([P, TOKEN_TILES, D_HEAD], BF16)
-        nc.sync.dma_start(out=cos_raw[:], in_=cos.rearrange("(t p) d -> p t d", p=P))
+        nc.sync.dma_start(out=cos_raw[:], in_=cos.rearrange("(p t) d -> p t d", p=P))
         sin_raw = keep.tile([P, TOKEN_TILES, D_HEAD], BF16)
-        nc.sync.dma_start(out=sin_raw[:], in_=sin.rearrange("(t p) d -> p t d", p=P))
+        nc.sync.dma_start(out=sin_raw[:], in_=sin.rearrange("(p t) d -> p t d", p=P))
         for t in range(1, TOKEN_TILES):
             load_x(t)
         for part in range(HEADS * D_HEAD // LOAD_COLUMNS):
@@ -115,19 +116,14 @@ def tile_attention_pa_kernel(tc, x, gamma, wq, wk, wv, sin, cos, out_0, out_1, o
             nc.vector.tensor_copy(out=gamma_col[:], in_=gamma_ps[:, :, 0:PASSES].rearrange("p j c -> p c j"))
 
         factor = keep.tile([P, TOKEN_TILES, 2, D_HEAD], BF16)
-        entries = factor[:].rearrange("p t s (i r) -> p t s i r", r=2)
-        cos_pairs = cos_raw[:].rearrange("p t (i r) -> p t i r", r=2)
+        crossed = factor[:, :, 1].rearrange("p t (i r) -> p t i r", r=2)
         sin_pairs = sin_raw[:].rearrange("p t (i r) -> p t i r", r=2)
         q_factor = keep.tile([P, TOKEN_TILES, 2, D_HEAD], F32)
 
         def rotary_tables():
-            for s, r, source, sign in (
-                (0, 0, cos_pairs, 1.0),
-                (0, 1, sin_pairs, 1.0),
-                (1, 0, sin_pairs, -1.0),
-                (1, 1, cos_pairs, 1.0),
-            ):
-                nc.scalar.activation(out=entries[:, :, s, :, r], in_=source[:, :, :, r], func=ACT.Copy, scale=sign)
+            nc.scalar.activation(out=factor[:, :, 0], in_=cos_raw[:], func=ACT.Copy, scale=1.0)
+            for r, sign in ((0, 1.0), (1, -1.0)):
+                nc.scalar.activation(out=crossed[:, :, :, r], in_=sin_pairs[:, :, :, 1 - r], func=ACT.Copy, scale=sign)
             nc.scalar.activation(out=q_factor[:], in_=factor[:], func=ACT.Copy, scale=D_HEAD**-0.5)
 
         x_codes = keep.tile([P, TOKEN_TILES, PASSES, P], U32, align_bytes=64)
@@ -268,27 +264,41 @@ def tile_attention_pa_kernel(tc, x, gamma, wq, wk, wv, sin, cos, out_0, out_1, o
                 )
 
         sums = {}
+        rotated = {}
 
         def project_q(ch, t):
             sums[(ch, t)] = psum.tile([P, BANK], F32, tag="bank", name="sums")
             project(sums[(ch, t)][:], ch, t, slice(0, BANK))
 
+        def add_products(engine, out, products):
+            engine.tensor_tensor(
+                out=out.rearrange("p n (i r) -> p n i r", r=2),
+                in0=products[:, 0].rearrange("p n (i r) -> p n i r", r=2),
+                in1=products[:, 1].rearrange("p n (i r) -> p n i r", r=2)[:, :, :, ::-1],
+                op=ALU.add,
+            )
+
         def finish_q(ch, t):
-            shape = [P, 2, HEADS_PER_CHUNK, PAIRS, 2]
-            products = rotary.tile([P, 2, HEADS_PER_CHUNK, D_HEAD], F32, tag="products", name="products")
+            shape = [P, 2, HEADS_PER_CHUNK, D_HEAD]
+            products = rotary.tile(shape, F32, tag="products", name="products")
             nc.vector.tensor_tensor(
-                out=products[:].rearrange("p s n (i r) -> p s n i r", r=2),
-                in0=sums[(ch, t)][:]
-                .rearrange("p (n i s) -> p s n i", s=2, i=PAIRS)
-                .unsqueeze(4)
-                .to_broadcast(shape),
-                in1=q_factor[:, t].rearrange("p s (i r) -> p s i r", r=2).unsqueeze(2).to_broadcast(shape),
+                out=products[:],
+                in0=sums[(ch, t)][:].rearrange("p (n d) -> p n d", d=D_HEAD).unsqueeze(1).to_broadcast(shape),
+                in1=q_factor[:, t].unsqueeze(2).to_broadcast(shape),
                 op=ALU.mult,
             )
-            q_rot = rotary.tile([P, HEADS_PER_CHUNK, D_HEAD], F32, tag="q_rot", name="q_rot", bufs=5)
-            nc.gpsimd.tensor_tensor(out=q_rot[:], in0=products[:, 0], in1=products[:, 1], op=ALU.add)
-            heads = out_0[0, ch * HEADS_PER_CHUNK : (ch + 1) * HEADS_PER_CHUNK, t * P : (t + 1) * P, :]
-            nc.sync.dma_start(out=heads.rearrange("h m d -> m h d"), in_=q_rot[:])
+            i = t % STORED_TILES
+            if i == 0:
+                rotated[ch] = rotary.tile(
+                    [P, HEADS_PER_CHUNK, STORED_TILES, D_HEAD], F32, tag="rotated", name="rotated", bufs=3
+                )
+            add_products(nc.gpsimd, rotated[ch][:, :, i], products[:])
+            heads = out_0[0, ch * HEADS_PER_CHUNK : (ch + 1) * HEADS_PER_CHUNK].rearrange("h (p t) d -> p h t d", p=P)
+            last = ch == Q_CHUNKS - 1 and t >= TOKEN_TILES - STORED_TILES
+            if last:
+                nc.sync.dma_start(out=heads[:, :, t], in_=rotated[ch][:, :, i])
+            elif i == STORED_TILES - 1:
+                nc.sync.dma_start(out=heads[:, :, t - i : t + 1], in_=rotated[ch][:])
 
         def project_kv(c):
             for t in range(TOKEN_TILES):
@@ -309,18 +319,17 @@ def tile_attention_pa_kernel(tc, x, gamma, wq, wk, wv, sin, cos, out_0, out_1, o
         def finish_kv():
             products = rotary.tile([P, 2, TOKEN_TILES, D_HEAD], F32, tag="products", name="products")
             for t in range(TOKEN_TILES):
-                shape = [P, 2, PAIRS, 2]
                 nc.vector.tensor_tensor(
-                    out=products[:, :, t].rearrange("p s (i r) -> p s i r", r=2),
-                    in0=sums[(KV, t)][:, 0:D_HEAD].rearrange("p (i s) -> p s i", s=2).unsqueeze(3).to_broadcast(shape),
-                    in1=factor[:, t].rearrange("p s (i r) -> p s i r", r=2),
+                    out=products[:, :, t],
+                    in0=sums[(KV, t)][:, 0:D_HEAD].unsqueeze(1).to_broadcast([P, 2, D_HEAD]),
+                    in1=factor[:, t],
                     op=ALU.mult,
                 )
                 nc.scalar.copy(out=v_copy[:, t], in_=sums[(KV, t)][:, D_HEAD:KV_WIDTH])
-            nc.sync.dma_start(out=out_2[0].rearrange("(t m) d -> m t d", m=P), in_=v_copy[:])
-            k_rot = rotary.tile([P, TOKEN_TILES, D_HEAD], F32, tag="q_rot", name="k_rot", bufs=5)
-            nc.vector.tensor_tensor(out=k_rot[:], in0=products[:, 0], in1=products[:, 1], op=ALU.add)
-            nc.sync.dma_start(out=out_1[0].rearrange("(t m) d -> m t d", m=P), in_=k_rot[:])
+            nc.sync.dma_start(out=out_2[0].rearrange("(p t) d -> p t d", p=P), in_=v_copy[:])
+            k_rot = rotary.tile([P, TOKEN_TILES, D_HEAD], F32, tag="k_rot", name="k_rot", bufs=1)
+            add_products(nc.vector, k_rot[:], products[:])
+            nc.sync.dma_start(out=out_1[0].rearrange("(p t) d -> p t d", p=P), in_=k_rot[:])
 
         banks = {}
         partial = {}
@@ -335,8 +344,8 @@ def tile_attention_pa_kernel(tc, x, gamma, wq, wk, wv, sin, cos, out_0, out_1, o
         partial[2] = fold_and_square(2)
         banks[1] = normalise_and_transpose(1, moments[1][0], moments[1][1])
         xn[0] = scale(0, banks[0])
-        moments[2] = scalar_moments(partial[2][0], partial[2][1])
         quantise_x(0, xn[0])
+        moments[2] = scalar_moments(partial[2][0], partial[2][1])
         partial[3] = fold_and_square(3)
         for c in range(3):
             regroup(0, c)
@@ -349,11 +358,11 @@ def tile_attention_pa_kernel(tc, x, gamma, wq, wk, wv, sin, cos, out_0, out_1, o
         xn[2] = scale(2, banks[2])
         quantise(0, 0)
         quantise_x(2, xn[2])
-        xn[3] = scale(3, banks[3])
         quantise(0, 1)
-        quantise_x(3, xn[3])
+        xn[3] = scale(3, banks[3])
         quantise(0, 2)
         quantise(0, 3)
+        quantise_x(3, xn[3])
         later = [(ch, c) for ch in range(1, CHUNKS) for c in range(PASSES)]
         for unit in later[:LEAD]:
             regroup(unit[0], unit[1])

from contextlib import ExitStack

import concourse.mybir as mybir
from concourse.masks import make_identity

F32 = mybir.dt.float32
BF16 = mybir.dt.bfloat16
U32 = mybir.dt.uint32
U8 = mybir.dt.uint8
FP8X4 = mybir.dt.float8_e4m3fn_x4
ALU = mybir.AluOpType
ACT = mybir.ActivationFunctionType
AXIS = mybir.AxisListType

P = 128
PACK = 4
K_PASS = P * PACK
TOKENS = 512
D_MODEL = 2048
HEADS = 16
D_HEAD = 128
EPS = 1e-5

TOKEN_TILES = TOKENS // P
PASSES = D_MODEL // K_PASS
ROW_GROUPS = D_MODEL // P
PAIRS = D_HEAD // 2
BANK = 512
Q_CHUNKS = HEADS * D_HEAD // BANK
HEADS_PER_CHUNK = BANK // D_HEAD
KV = Q_CHUNKS
CHUNKS = Q_CHUNKS + 1
KV_WIDTH = 2 * D_HEAD
STORED_TILES = 2
LOAD_COLUMNS = 2 * BANK
LEAD = 3
RUN = 4
BN_TILES = 2
NORM_PASSES = 2
VECTOR_UNITS = ((1, 2),)

FLOPS = 2 * TOKENS * D_MODEL * (HEADS * D_HEAD + KV_WIDTH)


def tile_attention_pa_kernel(tc, x, gamma, wq, wk, wv, sin, cos, out_0, out_1, out_2):
    nc = tc.nc
    with ExitStack() as ctx:
        keep = ctx.enter_context(tc.tile_pool(name="keep", bufs=1))
        small = ctx.enter_context(tc.tile_pool(name="small", bufs=4))
        rows = ctx.enter_context(tc.tile_pool(name="rows", bufs=2))
        regrouped = ctx.enter_context(tc.tile_pool(name="regrouped", bufs=8))
        coded = ctx.enter_context(tc.tile_pool(name="coded", bufs=3))
        rotary = ctx.enter_context(tc.tile_pool(name="rotary", bufs=3))
        psum = ctx.enter_context(tc.psum_pool(name="psum", bufs=8))
        ctx.enter_context(tc.manual_schedule())

        x_tiles = x.rearrange("b (p t) k -> (b t) p k", p=P)
        x_raw = {}

        def load_x(t, parts=1):
            x_raw[t] = keep.tile([P, D_MODEL], BF16, name="x_raw%d" % t)
            width = D_MODEL // parts
            for i in range(parts):
                features = slice(i * width, (i + 1) * width)
                nc.sync.dma_start(out=x_raw[t][:, features], in_=x_tiles[t][:, features])

        wq_passes = wq.rearrange("(c p j) n -> c p j n", j=PACK, p=P)
        wq_raw = {}

        def load_wq(part, c):
            wq_raw[(part, c)] = keep.tile([P, PACK, LOAD_COLUMNS], BF16, name="wq_raw%d_%d" % (part, c))
            columns = slice(part * LOAD_COLUMNS, (part + 1) * LOAD_COLUMNS)
            nc.sync.dma_start(out=wq_raw[(part, c)][:], in_=wq_passes[c][:, :, columns])

        gamma_rows = keep.tile([P, K_PASS], BF16)
        nc.vector.memset(gamma_rows[:], 0.0)
        load_x(0, 4)
        nc.sync.dma_start(out=gamma_rows[0:PASSES, :], in_=gamma.rearrange("(c f) -> c f", f=K_PASS))
        cos_raw = keep.tile([P, TOKEN_TILES, D_HEAD], BF16)
        nc.sync.dma_start(out=cos_raw[:], in_=cos.rearrange("(p t) d -> p t d", p=P))
        sin_raw = keep.tile([P, TOKEN_TILES, D_HEAD], BF16)
        nc.sync.dma_start(out=sin_raw[:], in_=sin.rearrange("(p t) d -> p t d", p=P))
        for t in range(1, TOKEN_TILES):
            load_x(t)
        for part in range(HEADS * D_HEAD // LOAD_COLUMNS):
            for c in range(PASSES):
                load_wq(part, c)
        kv_raw = keep.tile([P, PASSES, 2, PACK, D_HEAD], BF16)
        for s, weight in enumerate((wk, wv)):
            nc.sync.dma_start(
                out=kv_raw[:, :, s].rearrange("p c j n -> p c (j n)"),
                in_=weight.rearrange("(c p j) n -> p c (j n)", j=PACK, p=P),
            )

        ident_bf16 = keep.tile([P, P], BF16)
        make_identity(nc, ident_bf16[:])
        ident_f32 = keep.tile([P, P], F32)
        make_identity(nc, ident_f32[:])
        minus_half = keep.tile([P, 1], F32)
        nc.gpsimd.memset(minus_half[:], -0.5)
        one = keep.tile([P, 1], F32)
        nc.vector.memset(one[:], 1.0)
        table_warm = keep.tile([P, 1], F32)
        nc.scalar.activation(out=table_warm[:], in_=one[:], func=ACT.Square)
        mean_weights = keep.tile([P, P], BF16)
        nc.vector.tensor_scalar(
            out=mean_weights[:], in0=ident_bf16[:], scalar1=-1.0 / D_MODEL, scalar2=None, op0=ALU.mult
        )
        gamma_ps = psum.tile([P, PACK, P], BF16, tag="bank", name="gamma_ps")
        gamma_quads = gamma_rows[:].rearrange("q (p j) -> q j p", j=PACK)
        for j in range(PACK):
            nc.tensor.transpose(gamma_ps[:, j, :], gamma_quads[:, j, :], ident_bf16[:])
        gamma_col = keep.tile([P, PASSES, PACK], F32)

        def take_gamma():
            nc.vector.tensor_copy(out=gamma_col[:], in_=gamma_ps[:, :, 0:PASSES].rearrange("p j c -> p c j"))

        factor = keep.tile([P, TOKEN_TILES, 2, D_HEAD], BF16)
        crossed = factor[:, :, 1].rearrange("p t (i r) -> p t i r", r=2)
        sin_pairs = sin_raw[:].rearrange("p t (i r) -> p t i r", r=2)
        q_factor = keep.tile([P, TOKEN_TILES, 2, D_HEAD], F32)

        def rotary_tables():
            nc.scalar.activation(out=factor[:, :, 0], in_=cos_raw[:], func=ACT.Copy, scale=1.0)
            for r, sign in ((0, 1.0), (1, -1.0)):
                nc.scalar.activation(out=crossed[:, :, :, r], in_=sin_pairs[:, :, :, 1 - r], func=ACT.Copy, scale=sign)
            nc.scalar.activation(out=q_factor[:], in_=factor[:], func=ACT.Copy, scale=D_HEAD**-0.5)

        x_codes = keep.tile([P, TOKEN_TILES, PASSES, P], U32, align_bytes=64)
        x_scales = keep.tile([P, TOKEN_TILES, PASSES, P], U8, align_bytes=64)
        widths = [BANK] * Q_CHUNKS + [KV_WIDTH]
        w_codes = {}
        w_scales = {}

        def vector_moments(t):
            stats = small.tile([P, PASSES, 6], F32, name="stats")
            for c in range(PASSES):
                nc.vector.bn_stats(out=stats[:, c], in_=x_raw[t][:, c * K_PASS : (c + 1) * K_PASS])
            moments = small.tile([P, 2], F32, name="moments")
            nc.vector.bn_aggr(out=moments[:], in_=stats[:].rearrange("p c s -> p (c s)"))
            var_eps = small.tile([P, 1], F32, name="var_eps")
            nc.vector.tensor_scalar(out=var_eps[:], in0=moments[:, 1:2], scalar1=EPS, scalar2=None, op0=ALU.add)
            minus_mean = small.tile([P, 1], F32, name="minus_mean")
            nc.vector.tensor_scalar(out=minus_mean[:], in0=moments[:, 0:1], scalar1=-1.0, scalar2=None, op0=ALU.mult)
            return minus_mean, var_eps

        def fold_and_square(t):
            folded = psum.tile([P, P], F32, tag="bank", name="folded")
            for g in range(ROW_GROUPS):
                nc.tensor.matmul(
                    folded[:],
                    lhsT=mean_weights[:],
                    rhs=x_raw[t][:, g * P : (g + 1) * P],
                    start=(g == 0),
                    stop=(g == ROW_GROUPS - 1),
                )
            squares = keep.tile([P, D_MODEL], BF16, name="squares")
            sum_sq = small.tile([P, 1], F32, name="sum_sq")
            nc.scalar.activation(out=squares[:], in_=x_raw[t][:], func=ACT.Square, accum_out=sum_sq[:])
            return folded, sum_sq

        def scalar_moments(folded, sum_sq):
            minus_mean = small.tile([P, 1], F32, name="minus_mean")
            nc.vector.tensor_reduce(out=minus_mean[:], in_=folded[:], axis=AXIS.X, op=ALU.add)
            shift = small.tile([P, 1], F32, name="shift")
            nc.vector.tensor_scalar(
                out=shift[:], in0=minus_mean[:], scalar1=minus_mean[:, 0:1], scalar2=EPS, op0=ALU.mult, op1=ALU.subtract
            )
            var_eps = small.tile([P, 1], F32, name="var_eps")
            nc.gpsimd.tensor_scalar(
                out=var_eps[:], in0=sum_sq[:], scalar1=1.0 / D_MODEL, scalar2=shift[:, 0:1], op0=ALU.mult, op1=ALU.subtract
            )
            return minus_mean, var_eps

        def normalise_and_transpose(t, minus_mean, var_eps):
            rstd = small.tile([P, 1], F32, name="rstd")
            nc.gpsimd.tensor_tensor(out=rstd[:], in0=var_eps[:], in1=minus_half[:], op=ALU.pow)
            centred = rows.tile([P, D_MODEL], F32, name="centred")
            engine = nc.gpsimd
            passes = 1 if t == 0 else NORM_PASSES
            banks = []
            for c in range(PASSES):
                if c % passes == 0:
                    features = slice(c * K_PASS, (c + passes) * K_PASS)
                    engine.tensor_scalar(
                        out=centred[:, features].rearrange("q (c j p) -> q c j p", j=PACK, p=P),
                        in0=x_raw[t][:, features].rearrange("q (c p j) -> q c j p", j=PACK, p=P),
                        scalar1=minus_mean[:, 0:1],
                        scalar2=rstd[:, 0:1],
                        op0=ALU.add,
                        op1=ALU.mult,
                    )
                flipped = psum.tile([P, PACK, P], F32, tag="bank", name="flipped")
                for j in range(PACK):
                    g = c * PACK + j
                    nc.tensor.transpose(flipped[:, j, :], centred[:, g * P : (g + 1) * P], ident_f32[:])
                banks.append(flipped)
            return banks

        def scale(t, banks):
            xn = rows.tile([P, PASSES, P, PACK], BF16, align_bytes=64, name="xn")
            for c in range(PASSES):
                nc.vector.tensor_tensor(
                    out=xn[:, c, :, :],
                    in0=banks[c][:].rearrange("p j m -> p m j"),
                    in1=gamma_col[:, c, :].unsqueeze(1).to_broadcast([P, P, PACK]),
                    op=ALU.mult,
                )
            return xn

        def quantise_x(t, xn):
            nc.vector.quantize_mx(
                out=x_codes[:, t].rearrange("p c m -> p (c m)").bitcast(FP8X4),
                scales=x_scales[:, t].rearrange("p c m -> p (c m)"),
                in_=xn[:].rearrange("p c m j -> p (c m j)"),
            )

        grouped = {}

        def loaded_rows(ch, c):
            part, first = divmod(ch * BANK, LOAD_COLUMNS)
            return wq_raw[(part, c)][:, :, first : first + BANK]

        def regroup(ch, c):
            grouped[(ch, c)] = regrouped.tile(
                [P, widths[ch], PACK], BF16, tag="grouped", align_bytes=64, name="grouped"
            )
            if (ch, c) in VECTOR_UNITS:
                nc.vector.tensor_copy(
                    out=grouped[(ch, c)][:].rearrange("p (a i) j -> p a j i", i=RUN),
                    in_=loaded_rows(ch, c).rearrange("p j (a i) -> p a j i", i=RUN),
                )
            elif ch == KV:
                nc.scalar.copy(
                    out=grouped[(ch, c)][:].rearrange("p (s a i) j -> p s a j i", s=2, i=RUN),
                    in_=kv_raw[:, c].rearrange("p s j (a i) -> p s a j i", i=RUN),
                )
            else:
                nc.scalar.copy(
                    out=grouped[(ch, c)][:].rearrange("p (a i) j -> p a j i", i=RUN),
                    in_=loaded_rows(ch, c).rearrange("p j (a i) -> p a j i", i=RUN),
                )

        def quantise(ch, c):
            if c == 0:
                w_codes[ch] = coded.tile([P, PASSES, widths[ch]], U32, tag="codes", align_bytes=64, name="w_codes")
                w_scales[ch] = coded.tile([P, PASSES, widths[ch]], U8, tag="scales", align_bytes=64, name="w_scales")
            nc.vector.quantize_mx(
                out=w_codes[ch][:, c, :].bitcast(FP8X4),
                scales=w_scales[ch][:, c, :],
                in_=grouped[(ch, c)][:].rearrange("p n j -> p (n j)"),
            )

        def project(out, ch, t, columns):
            for c in range(PASSES):
                nc.tensor.matmul_mx(
                    out=out,
                    lhsT=x_codes[:, t, c, :].bitcast(FP8X4),
                    lhsT_scale=x_scales[:, t, c, :],
                    rhs=w_codes[ch][:, c, columns].bitcast(FP8X4),
                    rhs_scale=w_scales[ch][:, c, columns],
                    start=(c == 0),
                    stop=(c == PASSES - 1),
                )

        sums = {}
        rotated = {}

        def project_q(ch, t):
            sums[(ch, t)] = psum.tile([P, BANK], F32, tag="bank", name="sums")
            project(sums[(ch, t)][:], ch, t, slice(0, BANK))

        def add_products(engine, out, products):
            engine.tensor_tensor(
                out=out.rearrange("p n (i r) -> p n i r", r=2),
                in0=products[:, 0].rearrange("p n (i r) -> p n i r", r=2),
                in1=products[:, 1].rearrange("p n (i r) -> p n i r", r=2)[:, :, :, ::-1],
                op=ALU.add,
            )

        def finish_q(ch, t):
            shape = [P, 2, HEADS_PER_CHUNK, D_HEAD]
            products = rotary.tile(shape, F32, tag="products", name="products")
            nc.vector.tensor_tensor(
                out=products[:],
                in0=sums[(ch, t)][:].rearrange("p (n d) -> p n d", d=D_HEAD).unsqueeze(1).to_broadcast(shape),
                in1=q_factor[:, t].unsqueeze(2).to_broadcast(shape),
                op=ALU.mult,
            )
            i = t % STORED_TILES
            if i == 0:
                rotated[ch] = rotary.tile(
                    [P, HEADS_PER_CHUNK, STORED_TILES, D_HEAD], F32, tag="rotated", name="rotated", bufs=3
                )
            add_products(nc.gpsimd, rotated[ch][:, :, i], products[:])
            heads = out_0[0, ch * HEADS_PER_CHUNK : (ch + 1) * HEADS_PER_CHUNK].rearrange("h (p t) d -> p h t d", p=P)
            last = ch == Q_CHUNKS - 1 and t >= TOKEN_TILES - STORED_TILES
            if last:
                nc.sync.dma_start(out=heads[:, :, t], in_=rotated[ch][:, :, i])
            elif i == STORED_TILES - 1:
                nc.sync.dma_start(out=heads[:, :, t - i : t + 1], in_=rotated[ch][:])

        def project_kv(c):
            for t in range(TOKEN_TILES):
                if c == 0:
                    sums[(KV, t)] = psum.tile([P, KV_WIDTH], F32, tag="bank", name="sums")
                nc.tensor.matmul_mx(
                    out=sums[(KV, t)][:],
                    lhsT=x_codes[:, t, c, :].bitcast(FP8X4),
                    lhsT_scale=x_scales[:, t, c, :],
                    rhs=w_codes[KV][:, c, :].bitcast(FP8X4),
                    rhs_scale=w_scales[KV][:, c, :],
                    start=(c == 0),
                    stop=(c == PASSES - 1),
                )

        v_copy = keep.tile([P, TOKEN_TILES, D_HEAD], F32)

        def finish_kv():
            products = rotary.tile([P, 2, TOKEN_TILES, D_HEAD], F32, tag="products", name="products")
            for t in range(TOKEN_TILES):
                nc.vector.tensor_tensor(
                    out=products[:, :, t],
                    in0=sums[(KV, t)][:, 0:D_HEAD].unsqueeze(1).to_broadcast([P, 2, D_HEAD]),
                    in1=factor[:, t],
                    op=ALU.mult,
                )
                nc.scalar.copy(out=v_copy[:, t], in_=sums[(KV, t)][:, D_HEAD:KV_WIDTH])
            nc.sync.dma_start(out=out_2[0].rearrange("(p t) d -> p t d", p=P), in_=v_copy[:])
            k_rot = rotary.tile([P, TOKEN_TILES, D_HEAD], F32, tag="k_rot", name="k_rot", bufs=1)
            add_products(nc.vector, k_rot[:], products[:])
            nc.sync.dma_start(out=out_1[0].rearrange("(p t) d -> p t d", p=P), in_=k_rot[:])

        banks = {}
        partial = {}
        rotary_tables()
        banks = {}
        partial = {}
        xn = {}
        moments = {0: vector_moments(0)}
        banks[0] = normalise_and_transpose(0, moments[0][0], moments[0][1])
        moments[1] = vector_moments(1)
        take_gamma()
        partial[2] = fold_and_square(2)
        banks[1] = normalise_and_transpose(1, moments[1][0], moments[1][1])
        xn[0] = scale(0, banks[0])
        quantise_x(0, xn[0])
        moments[2] = scalar_moments(partial[2][0], partial[2][1])
        partial[3] = fold_and_square(3)
        for c in range(3):
            regroup(0, c)
        banks[2] = normalise_and_transpose(2, moments[2][0], moments[2][1])
        xn[1] = scale(1, banks[1])
        moments[3] = scalar_moments(partial[3][0], partial[3][1])
        quantise_x(1, xn[1])
        banks[3] = normalise_and_transpose(3, moments[3][0], moments[3][1])
        regroup(0, 3)
        xn[2] = scale(2, banks[2])
        quantise(0, 0)
        quantise_x(2, xn[2])
        quantise(0, 1)
        xn[3] = scale(3, banks[3])
        quantise(0, 2)
        quantise(0, 3)
        quantise_x(3, xn[3])
        later = [(ch, c) for ch in range(1, CHUNKS) for c in range(PASSES)]
        for unit in later[:LEAD]:
            regroup(unit[0], unit[1])

        for t in range(TOKEN_TILES):
            project_q(0, t)
        for ch in range(Q_CHUNKS):
            for t in range(TOKEN_TILES):
                quantise(ch + 1, t)
                for unit in later[ch * PASSES + t + LEAD :][:1]:
                    regroup(unit[0], unit[1])
                finish_q(ch, t)
            if ch + 1 < KV:
                for t in range(TOKEN_TILES):
                    project_q(ch + 1, t)
        for c in range(PASSES):
            project_kv(c)
        finish_kv()
